import numpy as np
import ml_dtypes


def mxq(x, axis, fmt="e4m3"):
    dtype, down = {"e4m3": (ml_dtypes.float8_e4m3fn, 7), "e5m2": (ml_dtypes.float8_e5m2, 14)}[fmt]
    v = np.moveaxis(np.asarray(x, np.float32).astype(ml_dtypes.bfloat16).astype(np.float64), axis, -1)
    blocks = v.reshape(v.shape[:-1] + (-1, 32))
    amax = np.abs(blocks).max(-1, keepdims=True)
    byte = np.maximum(np.where(amax > 0, np.frexp(amax)[1] - 1 + 127, 0) - down, 1)
    scale = np.exp2(byte - 127.0)
    codes = (blocks / scale).astype(np.float32).astype(dtype).astype(np.float64)
    return np.moveaxis((codes * scale).reshape(v.shape), -1, axis)


WIDE = False


def mx_kscale(k):
    if not WIDE:
        return np.ones(k)
    levels = np.array([18, -18])
    if k % 512:
        return np.exp2(np.random.permutation(np.resize(levels, k // 32))).repeat(32)
    a = np.empty((k // 512, 16))
    for p in range(k // 512):
        a[p, :8] = np.random.permutation(np.resize(levels, 8))
        for g in range(8):
            far = levels[np.abs(levels - a[p, g]) >= 10]
            a[p, g + 8] = far[np.random.randint(len(far))]
    return np.exp2(a.ravel()).repeat(32)


BF16 = ml_dtypes.bfloat16


def bf(x):
    return np.asarray(x, np.float32).astype(BF16)


def f64(x):
    return np.asarray(x).astype(np.float64)


N, C, F, O, DEG = 2048, 512, 512, 40, 16


def draw_adj():
    hit = (np.random.random((N, N)) < 0.5 * DEG / N).astype(np.float64)
    wt = 0.5 + np.random.random((N, N))
    return np.clip(hit + hit.T + np.eye(N), 0.0, 1.0) * (wt + wt.T) * 0.5


def setup_inputs():
    u = mx_kscale(N)
    s = mx_kscale(N)
    v = mx_kscale(F)
    t = np.cbrt(u * u * s)
    h0 = bf(np.maximum(np.random.standard_normal((N, F)) * 3.4, 0.0))
    adj0 = bf(draw_adj())
    w0 = bf(np.random.standard_normal((F, F)) * 0.5 * DEG / np.sqrt(F))
    rw0 = bf(np.random.standard_normal((F, F)) * 0.5 / np.sqrt(F))
    b = bf(np.random.standard_normal(F) * 0.3)
    g = bf(np.random.standard_normal((N, F)) * np.exp2(np.random.randint(-6, 1, (N, 1))) * 4.0 / t[:, None] * v)
    a = f64(adj0)
    dis = np.sum(a, axis=1) ** -0.5
    nnz = np.maximum(np.sum(np.where(a > 0.0, 1.0, 0.0), axis=1), 1.0)
    agg = ((dis[:, None] * a * dis[None, :]) @ f64(h0)) / nnz[:, None]
    y = agg @ f64(w0) + f64(h0) @ f64(rw0) + f64(b)
    return {"h": bf(f64(h0) * t[:, None]),
            "adj": bf(a * t[:, None] / t[None, :]),
            "w": bf(f64(w0) / v),
            "rw": bf(f64(rw0) / v),
            "b": b,
            "y": np.asarray(y, np.float32),
            "dis": np.asarray(dis, np.float32),
            "nnz": np.asarray(nnz, np.float32),
            "grad_out": g}


def reference(h, adj, w, rw, b, y, dis, nnz, grad_out):
    dis, nnz = f64(dis), f64(nnz)
    dy = f64(grad_out) * np.where(f64(y) > 0.0, 1.0, 0.0)
    dz2 = dy * (dis / nnz)[:, None]
    da = mxq(f64(adj), 0, "e4m3").T @ mxq(dz2, 0, "e5m2")
    dp = da * dis[:, None]
    dz1 = np.concatenate([dp, dy], axis=1)
    wr = np.concatenate([f64(w), f64(rw)], axis=1)
    dh = mxq(dz1, 1, "e5m2") @ mxq(wr, 1, "e4m3").T
    dw = mxq(f64(h), 0, "e4m3").T @ mxq(dp, 0, "e5m2")
    return dh, dw

@@ -1,0 +1,265 @@
+from contextlib import ExitStack
+
+import concourse.mybir as mybir
+from concourse.masks import make_identity
+
+F32 = mybir.dt.float32
+BF16 = mybir.dt.bfloat16
+U32 = mybir.dt.uint32
+U8 = mybir.dt.uint8
+E4M3 = mybir.dt.float8_e4m3fn_x4
+E5M2 = mybir.dt.float8_e5m2_x4
+ALU = mybir.AluOpType
+COPY = mybir.ActivationFunctionType.Copy
+
+N, F = 2048, 512
+P, J = 128, 4
+GROUP = P * J
+G = N // GROUP
+HALF = 1024
+
+FLOPS = 2 * N * N * F + 2 * N * 2 * F * F + 2 * N * F * F
+BYTES = 2 * (N * F + N * N + 2 * F * F + N * F) + 4 * (N * F + 2 * N) + 4 * (N * F + F * F)
+
+
+def tile_sage_re_pb_v_kernel(tc, h, adj, w, rw, b, y, dis, nnz, grad_out, out_0, out_1):
+    nc = tc.nc
+    adj_v = adj.rearrange("(g p j) c -> g p j c", p=P, j=J)
+    y_v = y.rearrange("(g p j) o -> g p j o", p=P, j=J)
+    go_v = grad_out.rearrange("(g p j) o -> g p j o", p=P, j=J)
+    h_v = h.rearrange("(g p j) o -> g p j o", p=P, j=J)
+    w_v = [x.rearrange("(b p) o -> p b o", p=P) for x in (w, rw)]
+    out0_v = out_0.rearrange("(g p j) f -> g p j f", p=P, j=J)
+    out1_v = out_1.rearrange("(b p) f -> b p f", p=P)
+
+    with ExitStack() as ctx:
+        keep = ctx.enter_context(tc.tile_pool(name="keep", bufs=1))
+        work = ctx.enter_context(tc.tile_pool(name="work", bufs=2))
+        psum = ctx.enter_context(tc.psum_pool(name="psum", bufs=1))
+
+        ident = keep.tile([P, P], F32, name="ident")
+        make_identity(nc, ident[:])
+        dis_t = keep.tile([P, G, J], F32, name="dis_t")
+        nnz_t = keep.tile([P, G, J], F32, name="nnz_t")
+        rinv = keep.tile([P, G, J], F32, name="rinv")
+        ratio = keep.tile([P, G, J], F32, name="ratio")
+
+        y_t, go_t, adj_t, h_t, w_t = {}, {}, {}, {}, {}
+        dy, dz = {}, {}
+        dp_t = {}
+        grp = {}
+        codes = {}
+        bank = {}
+
+        def coded(key, bufs=None, tag=None):
+            c = (keep if bufs is None else work).tile([P, GROUP], U32, name="c_%s" % key, tag=tag or "c_%s" % key, align_bytes=256, bufs=bufs or 1)
+            s = (keep if bufs is None else work).tile([P, GROUP], U8, name="s_%s" % key, tag="s_" + (tag or key), align_bytes=256, bufs=bufs or 1)
+            codes[key] = (c, s)
+
+        def new_group(key):
+            grp[key] = work.tile([P, J * GROUP], BF16, name="g_%s" % key, tag="grp", align_bytes=256, bufs=7)
+            return grp[key]
+
+        def new_bank(i):
+            return psum.tile([P, 512], F32, name="bank%d" % i, tag="bank%d" % i)
+
+        def load_y(g, k):
+            t = work.tile([P, 2, F], F32, name="y_%d_%d" % (g, k), tag="y", bufs=4)
+            nc.sync.dma_start(out=t[:], in_=y_v[g][:, 2 * k : 2 * k + 2, :])
+            y_t[g, k] = t
+
+        def load_go(g):
+            t = work.tile([P, J, F], BF16, name="go_%d" % g, tag="rows", bufs=8)
+            nc.sync.dma_start(out=t[:], in_=go_v[g])
+            go_t[g] = t
+
+        def load_h(g):
+            t = work.tile([P, J, F], BF16, name="h_%d" % g, tag="rows", bufs=8)
+            nc.sync.dma_start(out=t[:], in_=h_v[g])
+            h_t[g] = t
+
+        def load_w(i):
+            t = work.tile([P, J, F], BF16, name="w_%d" % i, tag="rows", bufs=8)
+            nc.sync.dma_start(out=t[:], in_=w_v[i])
+            w_t[i] = t
+
+        def load_adj(hf, g):
+            t = work.tile([P, J, HALF], BF16, name="adj_%d_%d" % (hf, g), tag="adj", bufs=4)
+            nc.sync.dma_start(out=t[:], in_=adj_v[g][:, :, hf * HALF : (hf + 1) * HALF])
+            for k in range(2):
+                adj_t[2 * hf + k, g] = t[:, :, k * GROUP : (k + 1) * GROUP]
+
+        def load_adj_quarter(q, g):
+            t = work.tile([P, J, GROUP], BF16, name="adjq_%d_%d" % (q, g), tag="rows", bufs=8)
+            nc.sync.dma_start(out=t[:], in_=adj_v[g][:, :, q * GROUP : (q + 1) * GROUP])
+            adj_t[q, g] = t[:]
+
+        ENG = {k: "S" for k in ("dz0", "dz2", "a0_1", "a0_2", "a0_3", "a1_2", "a2_2", "a3_0", "a3_1", "dpJ3")}
+        ENG.update({"dz1": "V", "dz3": "V"})
+
+        def mask(g, k):
+            if k == 0:
+                dy[g] = work.tile([P, J, F], BF16, name="dy_%d" % g, tag="dy", bufs=2, align_bytes=64)
+            pair = slice(2 * k, 2 * k + 2)
+            nc.vector.scalar_tensor_tensor(out=dy[g][:, pair, :], in0=y_t[g, k][:], scalar=0.0, in1=go_t[g][:, pair, :], op0=ALU.is_gt, op1=ALU.mult)
+
+        def scale(g, t):
+            if t == 0:
+                dz[g] = work.tile([P, J, F], BF16, name="dz_%d" % g, tag="dz", bufs=2, align_bytes=64)
+            nc.vector.tensor_scalar(out=dz[g][:, t, :], in0=dy[g][:, t, :], scalar1=ratio[:, g, t : t + 1], scalar2=None, op0=ALU.mult)
+
+        def copy_on(engine, out, in_):
+            if engine == "V":
+                nc.vector.tensor_copy(out=out, in_=in_)
+            else:
+                nc.scalar.copy(out=out, in_=in_)
+
+        def group_rows(engine, key, src):
+            copy_on(engine, new_group(key)[:].rearrange("p (c i t) -> p c t i", i=4, t=J), src[:].rearrange("p t (c i) -> p c t i", i=4))
+
+        def group_adj(engine, q, g):
+            src = adj_t[q, g]
+            copy_on(engine, new_group("a%d_%d" % (q, g))[:].rearrange("p (t m j) -> p m j t", t=J, j=J), src.rearrange("p j (m t) -> p m j t", t=J))
+
+        def quant(key, fmt, bufs=None, tag=None):
+            coded(key, bufs, tag)
+            c, s = codes[key]
+            nc.vector.quantize_mx(out=c[:].bitcast(fmt), scales=s[:], in_=grp[key][:])
+
+        def turn(key, k, i, words):
+            bk = new_bank(i)
+            bank[key, k] = bk
+            for s in range(2):
+                for u in range(2):
+                    nc.tensor.transpose(bk[:, (2 * s + u) * P : (2 * s + u + 1) * P], words(2 * k + s, u), ident[:])
+
+        def pair_words(src):
+            words = src[:].bitcast(F32)
+            return lambda t, u: words[:, t, u : 256 : 2]
+
+        def turned(engine, key, k):
+            if k == 0:
+                new_group(key)
+            dst = grp[key][:, k * 1024 : (k + 1) * 1024].bitcast(F32).rearrange("p (s r u) -> p s r u", s=2, u=2)
+            copy_on(engine, dst, bank[key, k][:].rearrange("p (s u r) -> p s r u", s=2, u=2))
+
+        def mm(out, lhs, lfmt, cols, rhs, rfmt, start, stop):
+            nc.tensor.matmul_mx(
+                out=out[:], lhsT=lhs[0][:, cols].bitcast(lfmt), lhsT_scale=lhs[1][:, cols], rhs=rhs[0][:].bitcast(rfmt), rhs_scale=rhs[1][:], start=start, stop=stop
+            )
+
+        def da(q, g, t, i):
+            if g == 0:
+                bank["da", q, t] = new_bank(i)
+            mm(bank["da", q, t], codes["a%d_%d" % (q, g)], E4M3, slice(t * P, (t + 1) * P), codes["dz%d" % g], E5M2, g == 0, g == G - 1)
+
+        def dp_exit(q, t):
+            if t == 0:
+                dp_t[q] = work.tile([P, J, F], BF16, name="dp_%d" % q, tag="dp", bufs=2, align_bytes=64)
+            nc.scalar.activation(out=dp_t[q][:, t, :], in_=bank["da", q, t][:], func=COPY, scale=dis_t[:, q, t : t + 1])
+
+        def dh(q, t, i):
+            bank["dh", q, t] = new_bank(i)
+            cols = slice(t * P, (t + 1) * P)
+            mm(bank["dh", q, t], codes["dyT%d" % q], E5M2, cols, codes["w1"], E4M3, True, False)
+            mm(bank["dh", q, t], codes["dpT%d" % q], E5M2, cols, codes["w0"], E4M3, False, True)
+
+        o0 = {}
+
+        def dh_exit(engine, q, t):
+            if t % 2 == 0:
+                o0[q] = work.tile([P, 2, F], F32, name="o0_%d_%d" % (q, t), tag="o0", bufs=3)
+            copy_on(engine, o0[q][:, t % 2, :], bank["dh", q, t][:])
+            if t % 2 == 1:
+                nc.sync.dma_start(out=out0_v[q][:, t - 1 : t + 1, :], in_=o0[q][:])
+
+        def dw(q, ft, i):
+            if q == 0:
+                bank["dw", ft] = new_bank(i)
+            mm(bank["dw", ft], codes["h%d" % q], E4M3, slice(ft * P, (ft + 1) * P), codes["dpJ%d" % q], E5M2, q == 0, q == G - 1)
+
+        def dw_exit(engine, ft):
+            o1 = work.tile([P, F], F32, name="o1_%d" % ft, tag="o1", bufs=2)
+            copy_on(engine, o1[:], bank["dw", ft][:])
+            nc.sync.dma_start(out=out1_v[ft], in_=o1[:])
+
+        nc.scalar.dma_start(out=nnz_t[:], in_=nnz.rearrange("(g p j) -> p g j", p=P, j=J))
+        nc.scalar.dma_start(out=dis_t[:], in_=dis.rearrange("(g p j) -> p g j", p=P, j=J))
+        load_adj_quarter(0, 0)
+        for g in range(G):
+            load_y(g, 0)
+            load_go(g)
+            load_y(g, 1)
+            if g > 0:
+                load_adj_quarter(0, g)
+        for i in range(2):
+            load_w(i)
+        for g in range(G):
+            load_adj_quarter(1, g)
+        for g in range(G):
+            load_adj(1, g)
+        for g in range(G):
+            load_h(g)
+        nc.vector.reciprocal(out=rinv[:], in_=nnz_t[:])
+        nc.vector.tensor_tensor(out=ratio[:], in0=dis_t[:], in1=rinv[:], op=ALU.mult)
+
+        def adj_unit(q, g):
+            key = "a%d_%d" % (q, g)
+            group_adj(ENG.get(key, "V"), q, g)
+            quant(key, E4M3, 10, "ca")
+
+        for g in range(G):
+            mask(g, 0)
+            mask(g, 1)
+            for t in range(J):
+                scale(g, t)
+            group_rows(ENG.get("dz%d" % g, "S"), "dz%d" % g, dz[g])
+            quant("dz%d" % g, E5M2)
+            adj_unit(0, g)
+            for t in range(J):
+                da(0, g, t, t)
+            turn("dyT%d" % g, 0, 6, pair_words(dy[g]))
+            turn("dyT%d" % g, 1, 7, pair_words(dy[g]))
+            turned("S", "dyT%d" % g, 0)
+            turned("V" if g == 0 else "S", "dyT%d" % g, 1)
+            quant("dyT%d" % g, E5M2)
+        for i in range(2):
+            for k in range(2):
+                turn("w%d" % i, k, 4 + k, pair_words(w_t[i]))
+                turned("S", "w%d" % i, k)
+            quant("w%d" % i, E4M3)
+
+        def finish(q):
+            for k in range(2):
+                turn("dpT%d" % q, k, 6 + k, pair_words(dp_t[q]))
+                turned("SV"[k], "dpT%d" % q, k)
+            quant("dpT%d" % q, E5M2, 2, "cdpT")
+            for t in range(J):
+                dh(q, t, (6, 7)[t % 2])
+                dh_exit("SV"[t % 2] if q == 3 else "S", q, t)
+
+        def row_part(q):
+            group_rows(ENG.get("dpJ%d" % q, "V"), "dpJ%d" % q, dp_t[q])
+            quant("dpJ%d" % q, E5M2)
+            group_rows(ENG.get("h%d" % q, "V"), "h%d" % q, h_t[q])
+            quant("h%d" % q, E4M3)
+
+        DAB = ((0, 1, 2, 3), (4, 5, 4, 5), (0, 1, 2, 3), (4, 5, 4, 5))
+        for q in range(G):
+            for t in range(J):
+                if q > 0:
+                    for g in range(G):
+                        da(q, g, t, DAB[q][t])
+                dp_exit(q, t)
+            finish(q)
+            if q < 3:
+                for g in range(G):
+                    adj_unit(q + 1, g)
+            if q > 0:
+                row_part(q - 1)
+        row_part(3)
+        for q in range(G):
+            for ft in range(4):
+                dw(q, ft, ft)
+        for ft in range(4):
+            dw_exit("VS"[ft % 2], ft)

@@ -30,12 +30,13 @@ def tile_sage_re_pb_v_kernel(tc, h, adj, w, rw, b, y, dis, nnz, grad_out, out_0,
     h_v = h.rearrange("(g p j) o -> g p j o", p=P, j=J)
     w_v = [x.rearrange("(b p) o -> p b o", p=P) for x in (w, rw)]
     out0_v = out_0.rearrange("(g p j) f -> g p j f", p=P, j=J)
-    out1_v = out_1.rearrange("(b p) f -> b p f", p=P)
+    out1_v = out_1.rearrange("(b p) f -> p b f", p=P)
 
     with ExitStack() as ctx:
         keep = ctx.enter_context(tc.tile_pool(name="keep", bufs=1))
         work = ctx.enter_context(tc.tile_pool(name="work", bufs=2))
         psum = ctx.enter_context(tc.psum_pool(name="psum", bufs=1))
+        ctx.enter_context(tc.manual_schedule())
 
         ident = keep.tile([P, P], F32, name="ident")
         make_identity(nc, ident[:])
@@ -57,7 +58,7 @@ def tile_sage_re_pb_v_kernel(tc, h, adj, w, rw, b, y, dis, nnz, grad_out, out_0,
             codes[key] = (c, s)
 
         def new_group(key):
-            grp[key] = work.tile([P, J * GROUP], BF16, name="g_%s" % key, tag="grp", align_bytes=256, bufs=7)
+            grp[key] = work.tile([P, J * GROUP], BF16, name="g_%s" % key, tag="grp", align_bytes=256, bufs=8)
             return grp[key]
 
         def new_bank(i):
@@ -68,18 +69,18 @@ def tile_sage_re_pb_v_kernel(tc, h, adj, w, rw, b, y, dis, nnz, grad_out, out_0,
             nc.sync.dma_start(out=t[:], in_=y_v[g][:, 2 * k : 2 * k + 2, :])
             y_t[g, k] = t
 
-        def load_go(g):
-            t = work.tile([P, J, F], BF16, name="go_%d" % g, tag="rows", bufs=8)
-            nc.sync.dma_start(out=t[:], in_=go_v[g])
-            go_t[g] = t
+        def load_go(g, k):
+            t = work.tile([P, 2, F], BF16, name="go_%d_%d" % (g, k), tag="go", bufs=4)
+            nc.sync.dma_start(out=t[:], in_=go_v[g][:, 2 * k : 2 * k + 2, :])
+            go_t[g, k] = t
 
         def load_h(g):
-            t = work.tile([P, J, F], BF16, name="h_%d" % g, tag="rows", bufs=8)
+            t = work.tile([P, J, F], BF16, name="h_%d" % g, tag="rows", bufs=7)
             nc.sync.dma_start(out=t[:], in_=h_v[g])
             h_t[g] = t
 
         def load_w(i):
-            t = work.tile([P, J, F], BF16, name="w_%d" % i, tag="rows", bufs=8)
+            t = work.tile([P, J, F], BF16, name="w_%d" % i, tag="rows", bufs=7)
             nc.sync.dma_start(out=t[:], in_=w_v[i])
             w_t[i] = t
 
@@ -90,18 +91,16 @@ def tile_sage_re_pb_v_kernel(tc, h, adj, w, rw, b, y, dis, nnz, grad_out, out_0,
                 adj_t[2 * hf + k, g] = t[:, :, k * GROUP : (k + 1) * GROUP]
 
         def load_adj_quarter(q, g):
-            t = work.tile([P, J, GROUP], BF16, name="adjq_%d_%d" % (q, g), tag="rows", bufs=8)
+            t = work.tile([P, J, GROUP], BF16, name="adjq_%d_%d" % (q, g), tag="rows", bufs=7)
             nc.sync.dma_start(out=t[:], in_=adj_v[g][:, :, q * GROUP : (q + 1) * GROUP])
             adj_t[q, g] = t[:]
 
-        ENG = {k: "S" for k in ("dz0", "dz2", "a0_1", "a0_2", "a0_3", "a1_2", "a2_2", "a3_0", "a3_1", "dpJ3")}
-        ENG.update({"dz1": "V", "dz3": "V"})
 
         def mask(g, k):
             if k == 0:
                 dy[g] = work.tile([P, J, F], BF16, name="dy_%d" % g, tag="dy", bufs=2, align_bytes=64)
             pair = slice(2 * k, 2 * k + 2)
-            nc.vector.scalar_tensor_tensor(out=dy[g][:, pair, :], in0=y_t[g, k][:], scalar=0.0, in1=go_t[g][:, pair, :], op0=ALU.is_gt, op1=ALU.mult)
+            nc.vector.scalar_tensor_tensor(out=dy[g][:, pair, :], in0=y_t[g, k][:], scalar=0.0, in1=go_t[g, k][:], op0=ALU.is_gt, op1=ALU.mult)
 
         def scale(g, t):
             if t == 0:
@@ -168,7 +167,7 @@ def tile_sage_re_pb_v_kernel(tc, h, adj, w, rw, b, y, dis, nnz, grad_out, out_0,
 
         def dh_exit(engine, q, t):
             if t % 2 == 0:
-                o0[q] = work.tile([P, 2, F], F32, name="o0_%d_%d" % (q, t), tag="o0", bufs=3)
+                o0[q] = work.tile([P, 2, F], F32, name="o0_%d_%d" % (q, t), tag="o0", bufs=4)
             copy_on(engine, o0[q][:, t % 2, :], bank["dh", q, t][:])
             if t % 2 == 1:
                 nc.sync.dma_start(out=out0_v[q][:, t - 1 : t + 1, :], in_=o0[q][:])
@@ -179,22 +178,25 @@ def tile_sage_re_pb_v_kernel(tc, h, adj, w, rw, b, y, dis, nnz, grad_out, out_0,
             mm(bank["dw", ft], codes["h%d" % q], E4M3, slice(ft * P, (ft + 1) * P), codes["dpJ%d" % q], E5M2, q == 0, q == G - 1)
 
         def dw_exit(engine, ft):
-            o1 = work.tile([P, F], F32, name="o1_%d" % ft, tag="o1", bufs=2)
-            copy_on(engine, o1[:], bank["dw", ft][:])
-            nc.sync.dma_start(out=out1_v[ft], in_=o1[:])
+            if ft % 2 == 0:
+                o0["w"] = work.tile([P, 2, F], F32, name="o1_%d" % ft, tag="o0", bufs=4)
+            copy_on(engine, o0["w"][:, ft % 2, :], bank["dw", ft][:])
+            if ft % 2 == 1:
+                nc.sync.dma_start(out=out1_v[:, ft - 1 : ft + 1, :], in_=o0["w"][:])
 
         nc.scalar.dma_start(out=nnz_t[:], in_=nnz.rearrange("(g p j) -> p g j", p=P, j=J))
         nc.scalar.dma_start(out=dis_t[:], in_=dis.rearrange("(g p j) -> p g j", p=P, j=J))
-        load_adj_quarter(0, 0)
         for g in range(G):
-            load_y(g, 0)
-            load_go(g)
-            load_y(g, 1)
-            if g > 0:
-                load_adj_quarter(0, g)
+            for k in range(2):
+                load_y(g, k)
+                load_go(g, k)
+        for g in (0, 1, 2, 3):
+            load_adj_quarter(0, g)
+        for g in (1, 0):
+            load_adj_quarter(1, g)
         for i in range(2):
             load_w(i)
-        for g in range(G):
+        for g in (2, 3):
             load_adj_quarter(1, g)
         for g in range(G):
             load_adj(1, g)
@@ -203,63 +205,116 @@ def tile_sage_re_pb_v_kernel(tc, h, adj, w, rw, b, y, dis, nnz, grad_out, out_0,
         nc.vector.reciprocal(out=rinv[:], in_=nnz_t[:])
         nc.vector.tensor_tensor(out=ratio[:], in0=dis_t[:], in1=rinv[:], op=ALU.mult)
 
-        def adj_unit(q, g):
-            key = "a%d_%d" % (q, g)
-            group_adj(ENG.get(key, "V"), q, g)
-            quant(key, E4M3, 10, "ca")
+        def adj_quant(q, g):
+            quant("a%d_%d" % (q, g), E4M3, 9, "ca")
 
-        for g in range(G):
-            mask(g, 0)
-            mask(g, 1)
+        def turn_pair(key, i0, src):
+            turn(key, 0, i0, pair_words(src))
+            turn(key, 1, i0 + 1, pair_words(src))
+
+        def turned_pair(engines, key):
+            turned(engines[0], key, 0)
+            turned(engines[1], key, 1)
+
+        for g in range(G + 1):
+            if g < G:
+                mask(g, 0)
+                mask(g, 1)
+                for t in range(J):
+                    scale(g, t)
+                turn_pair("dyT%d" % g, 6, dy[g])
+                group_rows("S", "dz%d" % g, dz[g])
+                turned_pair("SS", "dyT%d" % g)
+            if g > 0:
+                if g == G:
+                    group_adj("V", 0, 0)
+                quant("dz%d" % (g - 1), E5M2)
+                quant("dyT%d" % (g - 1), E5M2)
+        group_adj("S", 0, 1)
+        adj_quant(0, 0)
+        group_adj("V", 0, 2)
+        group_adj("S", 0, 3)
+        adj_quant(0, 1)
+        group_adj("V", 1, 0)
+        adj_quant(0, 2)
+        adj_quant(0, 3)
+        ORDER = (1, 0, 2, 3)
+
+        def da_pass(q, g, order):
             for t in range(J):
-                scale(g, t)
-            group_rows(ENG.get("dz%d" % g, "S"), "dz%d" % g, dz[g])
-            quant("dz%d" % g, E5M2)
-            adj_unit(0, g)
-            for t in range(J):
-                da(0, g, t, t)
-            turn("dyT%d" % g, 0, 6, pair_words(dy[g]))
-            turn("dyT%d" % g, 1, 7, pair_words(dy[g]))
-            turned("S", "dyT%d" % g, 0)
-            turned("V" if g == 0 else "S", "dyT%d" % g, 1)
-            quant("dyT%d" % g, E5M2)
-        for i in range(2):
-            for k in range(2):
-                turn("w%d" % i, k, 4 + k, pair_words(w_t[i]))
-                turned("S", "w%d" % i, k)
-            quant("w%d" % i, E4M3)
+                if g == order[0]:
+                    bank["da", q, t] = new_bank((0, 1, 4, 5)[t])
+                mm(bank["da", q, t], codes["a%d_%d" % (q, g)], E4M3, slice(t * P, (t + 1) * P), codes["dz%d" % g], E5M2, g == order[0], g == order[-1])
 
-        def finish(q):
-            for k in range(2):
-                turn("dpT%d" % q, k, 6 + k, pair_words(dp_t[q]))
-                turned("SV"[k], "dpT%d" % q, k)
-            quant("dpT%d" % q, E5M2, 2, "cdpT")
-            for t in range(J):
-                dh(q, t, (6, 7)[t % 2])
-                dh_exit("SV"[t % 2] if q == 3 else "S", q, t)
-
-        def row_part(q):
-            group_rows(ENG.get("dpJ%d" % q, "V"), "dpJ%d" % q, dp_t[q])
-            quant("dpJ%d" % q, E5M2)
-            group_rows(ENG.get("h%d" % q, "V"), "h%d" % q, h_t[q])
-            quant("h%d" % q, E4M3)
-
-        DAB = ((0, 1, 2, 3), (4, 5, 4, 5), (0, 1, 2, 3), (4, 5, 4, 5))
+        for g in range(3):
+            da_pass(0, g, (0, 1, 2, 3))
+        da_pass(0, 3, (0, 1, 2, 3))
+        group_adj("S", 1, 1)
         for q in range(G):
-            for t in range(J):
-                if q > 0:
-                    for g in range(G):
-                        da(q, g, t, DAB[q][t])
-                dp_exit(q, t)
-            finish(q)
-            if q < 3:
-                for g in range(G):
-                    adj_unit(q + 1, g)
+            n = q + 1
             if q > 0:
-                row_part(q - 1)
-        row_part(3)
-        for q in range(G):
+                dh_exit("S", q - 1, 0)
+                dh_exit("S", q - 1, 1)
+            for t in range(J):
+                dp_exit(q, t)
+            if q > 0:
+                for t in (2, 3):
+                    dh(q - 1, t, t)
+                    dh_exit("S", q - 1, t)
+            turn_pair("dpT%d" % q, 6, dp_t[q])
+            turned_pair("SS", "dpT%d" % q)
+            if q == 0:
+                for i in range(2):
+                    turn_pair("w%d" % i, (2, 6)[i], w_t[i])
+                turned_pair("SS", "w1")
+            if n + 1 < G:
+                group_adj("S", n + 1, 1)
+            if q == 2:
+                group_rows("S", "h0", h_t[0])
+            if n < G:
+                adj_quant(n, 1)
+                da_pass(n, 1, ORDER)
+                if q > 0:
+                    group_adj("V", n, 0)
+                    group_rows("V", "dpJ%d" % (q - 1), dp_t[q - 1])
+                adj_quant(n, 0)
+                da_pass(n, 0, ORDER)
+                group_adj("V", n, 2)
+                if q > 0:
+                    quant("dpJ%d" % (q - 1), E5M2)
+                if q == 0:
+                    turned_pair("VV", "w0")
+                group_adj("V", n, 3)
+                if q == 0:
+                    quant("w0", E4M3)
+                    quant("w1", E4M3)
+                adj_quant(n, 2)
+                quant("dpT%d" % q, E5M2, 2, "cdpT")
+                adj_quant(n, 3)
+                for t in (0, 1):
+                    dh(q, t, 2 + t)
+                da_pass(n, 2, ORDER)
+                da_pass(n, 3, ORDER)
+            else:
+                group_rows("V", "h1", h_t[1])
+                group_rows("V", "dpJ2", dp_t[2])
+                quant("h1", E4M3)
+                quant("h0", E4M3)
+                quant("dpJ2", E5M2)
+                group_rows("V", "h2", h_t[2])
+                group_rows("V", "dpJ3", dp_t[3])
+                quant("h2", E4M3)
+                group_rows("S", "h3", h_t[3])
+        DW = (4, 5, 0, 1)
+        quant("dpT3", E5M2, 2, "cdpT")
+        quant("dpJ3", E5M2)
+        quant("h3", E4M3)
+        for q in range(3):
             for ft in range(4):
-                dw(q, ft, ft)
+                dw(q, ft, DW[ft])
+        for t in range(J):
+            dh(3, t, (2, 3)[t % 2])
+            dh_exit("VS"[t % 2], 3, t)
         for ft in range(4):
+            dw(3, ft, DW[ft])
             dw_exit("VS"[ft % 2], ft)

from contextlib import ExitStack

import concourse.mybir as mybir
from concourse.masks import make_identity

F32 = mybir.dt.float32
BF16 = mybir.dt.bfloat16
U32 = mybir.dt.uint32
U8 = mybir.dt.uint8
E4M3 = mybir.dt.float8_e4m3fn_x4
E5M2 = mybir.dt.float8_e5m2_x4
ALU = mybir.AluOpType
COPY = mybir.ActivationFunctionType.Copy

N, F = 2048, 512
P, J = 128, 4
GROUP = P * J
G = N // GROUP
HALF = 1024

FLOPS = 2 * N * N * F + 2 * N * 2 * F * F + 2 * N * F * F
BYTES = 2 * (N * F + N * N + 2 * F * F + N * F) + 4 * (N * F + 2 * N) + 4 * (N * F + F * F)


def tile_sage_re_pb_v_kernel(tc, h, adj, w, rw, b, y, dis, nnz, grad_out, out_0, out_1):
    nc = tc.nc
    adj_v = adj.rearrange("(g p j) c -> g p j c", p=P, j=J)
    y_v = y.rearrange("(g p j) o -> g p j o", p=P, j=J)
    go_v = grad_out.rearrange("(g p j) o -> g p j o", p=P, j=J)
    h_v = h.rearrange("(g p j) o -> g p j o", p=P, j=J)
    w_v = [x.rearrange("(b p) o -> p b o", p=P) for x in (w, rw)]
    out0_v = out_0.rearrange("(g p j) f -> g p j f", p=P, j=J)
    out1_v = out_1.rearrange("(b p) f -> p b f", p=P)

    with ExitStack() as ctx:
        keep = ctx.enter_context(tc.tile_pool(name="keep", bufs=1))
        work = ctx.enter_context(tc.tile_pool(name="work", bufs=2))
        psum = ctx.enter_context(tc.psum_pool(name="psum", bufs=1))
        ctx.enter_context(tc.manual_schedule())

        ident = keep.tile([P, P], F32, name="ident")
        make_identity(nc, ident[:])
        dis_t = keep.tile([P, G, J], F32, name="dis_t")
        nnz_t = keep.tile([P, G, J], F32, name="nnz_t")
        rinv = keep.tile([P, G, J], F32, name="rinv")
        ratio = keep.tile([P, G, J], F32, name="ratio")

        y_t, go_t, adj_t, h_t, w_t = {}, {}, {}, {}, {}
        dy, dz = {}, {}
        dp_t = {}
        grp = {}
        codes = {}
        bank = {}

        def coded(key, bufs=None, tag=None):
            c = (keep if bufs is None else work).tile([P, GROUP], U32, name="c_%s" % key, tag=tag or "c_%s" % key, align_bytes=256, bufs=bufs or 1)
            s = (keep if bufs is None else work).tile([P, GROUP], U8, name="s_%s" % key, tag="s_" + (tag or key), align_bytes=256, bufs=bufs or 1)
            codes[key] = (c, s)

        def new_group(key):
            grp[key] = work.tile([P, J * GROUP], BF16, name="g_%s" % key, tag="grp", align_bytes=256, bufs=8)
            return grp[key]

        def new_bank(i):
            return psum.tile([P, 512], F32, name="bank%d" % i, tag="bank%d" % i)

        def load_y(g, k):
            t = work.tile([P, 2, F], F32, name="y_%d_%d" % (g, k), tag="y", bufs=4)
            nc.sync.dma_start(out=t[:], in_=y_v[g][:, 2 * k : 2 * k + 2, :])
            y_t[g, k] = t

        def load_go(g, k):
            t = work.tile([P, 2, F], BF16, name="go_%d_%d" % (g, k), tag="go", bufs=4)
            nc.sync.dma_start(out=t[:], in_=go_v[g][:, 2 * k : 2 * k + 2, :])
            go_t[g, k] = t

        def load_h(g):
            t = work.tile([P, J, F], BF16, name="h_%d" % g, tag="rows", bufs=7)
            nc.sync.dma_start(out=t[:], in_=h_v[g])
            h_t[g] = t

        def load_w(i):
            t = work.tile([P, J, F], BF16, name="w_%d" % i, tag="rows", bufs=7)
            nc.sync.dma_start(out=t[:], in_=w_v[i])
            w_t[i] = t

        def load_adj(hf, g):
            t = work.tile([P, J, HALF], BF16, name="adj_%d_%d" % (hf, g), tag="adj", bufs=4)
            nc.sync.dma_start(out=t[:], in_=adj_v[g][:, :, hf * HALF : (hf + 1) * HALF])
            for k in range(2):
                adj_t[2 * hf + k, g] = t[:, :, k * GROUP : (k + 1) * GROUP]

        def load_adj_quarter(q, g):
            t = work.tile([P, J, GROUP], BF16, name="adjq_%d_%d" % (q, g), tag="rows", bufs=7)
            nc.sync.dma_start(out=t[:], in_=adj_v[g][:, :, q * GROUP : (q + 1) * GROUP])
            adj_t[q, g] = t[:]


        def mask(g, k):
            if k == 0:
                dy[g] = work.tile([P, J, F], BF16, name="dy_%d" % g, tag="dy", bufs=2, align_bytes=64)
            pair = slice(2 * k, 2 * k + 2)
            nc.vector.scalar_tensor_tensor(out=dy[g][:, pair, :], in0=y_t[g, k][:], scalar=0.0, in1=go_t[g, k][:], op0=ALU.is_gt, op1=ALU.mult)

        def scale(g, t):
            if t == 0:
                dz[g] = work.tile([P, J, F], BF16, name="dz_%d" % g, tag="dz", bufs=2, align_bytes=64)
            nc.vector.tensor_scalar(out=dz[g][:, t, :], in0=dy[g][:, t, :], scalar1=ratio[:, g, t : t + 1], scalar2=None, op0=ALU.mult)

        def copy_on(engine, out, in_):
            if engine == "V":
                nc.vector.tensor_copy(out=out, in_=in_)
            else:
                nc.scalar.copy(out=out, in_=in_)

        def group_rows(engine, key, src):
            copy_on(engine, new_group(key)[:].rearrange("p (c i t) -> p c t i", i=4, t=J), src[:].rearrange("p t (c i) -> p c t i", i=4))

        def group_adj(engine, q, g):
            src = adj_t[q, g]
            copy_on(engine, new_group("a%d_%d" % (q, g))[:].rearrange("p (t m j) -> p m j t", t=J, j=J), src.rearrange("p j (m t) -> p m j t", t=J))

        def quant(key, fmt, bufs=None, tag=None):
            coded(key, bufs, tag)
            c, s = codes[key]
            nc.vector.quantize_mx(out=c[:].bitcast(fmt), scales=s[:], in_=grp[key][:])

        def turn(key, k, i, words):
            bk = new_bank(i)
            bank[key, k] = bk
            for s in range(2):
                for u in range(2):
                    nc.tensor.transpose(bk[:, (2 * s + u) * P : (2 * s + u + 1) * P], words(2 * k + s, u), ident[:])

        def pair_words(src):
            words = src[:].bitcast(F32)
            return lambda t, u: words[:, t, u : 256 : 2]

        def turned(engine, key, k):
            if k == 0:
                new_group(key)
            dst = grp[key][:, k * 1024 : (k + 1) * 1024].bitcast(F32).rearrange("p (s r u) -> p s r u", s=2, u=2)
            copy_on(engine, dst, bank[key, k][:].rearrange("p (s u r) -> p s r u", s=2, u=2))

        def mm(out, lhs, lfmt, cols, rhs, rfmt, start, stop):
            nc.tensor.matmul_mx(
                out=out[:], lhsT=lhs[0][:, cols].bitcast(lfmt), lhsT_scale=lhs[1][:, cols], rhs=rhs[0][:].bitcast(rfmt), rhs_scale=rhs[1][:], start=start, stop=stop
            )

        def da(q, g, t, i):
            if g == 0:
                bank["da", q, t] = new_bank(i)
            mm(bank["da", q, t], codes["a%d_%d" % (q, g)], E4M3, slice(t * P, (t + 1) * P), codes["dz%d" % g], E5M2, g == 0, g == G - 1)

        def dp_exit(q, t):
            if t == 0:
                dp_t[q] = work.tile([P, J, F], BF16, name="dp_%d" % q, tag="dp", bufs=2, align_bytes=64)
            nc.scalar.activation(out=dp_t[q][:, t, :], in_=bank["da", q, t][:], func=COPY, scale=dis_t[:, q, t : t + 1])

        def dh(q, t, i):
            bank["dh", q, t] = new_bank(i)
            cols = slice(t * P, (t + 1) * P)
            mm(bank["dh", q, t], codes["dyT%d" % q], E5M2, cols, codes["w1"], E4M3, True, False)
            mm(bank["dh", q, t], codes["dpT%d" % q], E5M2, cols, codes["w0"], E4M3, False, True)

        o0 = {}

        def dh_exit(engine, q, t):
            if t % 2 == 0:
                o0[q] = work.tile([P, 2, F], F32, name="o0_%d_%d" % (q, t), tag="o0", bufs=4)
            copy_on(engine, o0[q][:, t % 2, :], bank["dh", q, t][:])
            if t % 2 == 1:
                nc.sync.dma_start(out=out0_v[q][:, t - 1 : t + 1, :], in_=o0[q][:])

        def dw(q, ft, i):
            if q == 0:
                bank["dw", ft] = new_bank(i)
            mm(bank["dw", ft], codes["h%d" % q], E4M3, slice(ft * P, (ft + 1) * P), codes["dpJ%d" % q], E5M2, q == 0, q == G - 1)

        def dw_exit(engine, ft):
            if ft % 2 == 0:
                o0["w"] = work.tile([P, 2, F], F32, name="o1_%d" % ft, tag="o0", bufs=4)
            copy_on(engine, o0["w"][:, ft % 2, :], bank["dw", ft][:])
            if ft % 2 == 1:
                nc.sync.dma_start(out=out1_v[:, ft - 1 : ft + 1, :], in_=o0["w"][:])

        nc.scalar.dma_start(out=nnz_t[:], in_=nnz.rearrange("(g p j) -> p g j", p=P, j=J))
        nc.scalar.dma_start(out=dis_t[:], in_=dis.rearrange("(g p j) -> p g j", p=P, j=J))
        for g in range(G):
            for k in range(2):
                load_y(g, k)
                load_go(g, k)
        for g in (0, 1, 2, 3):
            load_adj_quarter(0, g)
        for g in (1, 0):
            load_adj_quarter(1, g)
        for i in range(2):
            load_w(i)
        for g in (2, 3):
            load_adj_quarter(1, g)
        for g in range(G):
            load_adj(1, g)
        for g in range(G):
            load_h(g)
        nc.vector.reciprocal(out=rinv[:], in_=nnz_t[:])
        nc.vector.tensor_tensor(out=ratio[:], in0=dis_t[:], in1=rinv[:], op=ALU.mult)

        def adj_quant(q, g):
            quant("a%d_%d" % (q, g), E4M3, 9, "ca")

        def turn_pair(key, i0, src):
            turn(key, 0, i0, pair_words(src))
            turn(key, 1, i0 + 1, pair_words(src))

        def turned_pair(engines, key):
            turned(engines[0], key, 0)
            turned(engines[1], key, 1)

        for g in range(G + 1):
            if g < G:
                mask(g, 0)
                mask(g, 1)
                for t in range(J):
                    scale(g, t)
                turn_pair("dyT%d" % g, 6, dy[g])
                group_rows("S", "dz%d" % g, dz[g])
                turned_pair("SS", "dyT%d" % g)
            if g > 0:
                if g == G:
                    group_adj("V", 0, 0)
                quant("dz%d" % (g - 1), E5M2)
                quant("dyT%d" % (g - 1), E5M2)
        group_adj("S", 0, 1)
        adj_quant(0, 0)
        group_adj("V", 0, 2)
        group_adj("S", 0, 3)
        adj_quant(0, 1)
        group_adj("V", 1, 0)
        adj_quant(0, 2)
        adj_quant(0, 3)
        ORDER = (1, 0, 2, 3)

        def da_pass(q, g, order):
            for t in range(J):
                if g == order[0]:
                    bank["da", q, t] = new_bank((0, 1, 4, 5)[t])
                mm(bank["da", q, t], codes["a%d_%d" % (q, g)], E4M3, slice(t * P, (t + 1) * P), codes["dz%d" % g], E5M2, g == order[0], g == order[-1])

        for g in range(3):
            da_pass(0, g, (0, 1, 2, 3))
        da_pass(0, 3, (0, 1, 2, 3))
        group_adj("S", 1, 1)
        for q in range(G):
            n = q + 1
            if q > 0:
                dh_exit("S", q - 1, 0)
                dh_exit("S", q - 1, 1)
            for t in range(J):
                dp_exit(q, t)
            if q > 0:
                for t in (2, 3):
                    dh(q - 1, t, t)
                    dh_exit("S", q - 1, t)
            turn_pair("dpT%d" % q, 6, dp_t[q])
            turned_pair("SS", "dpT%d" % q)
            if q == 0:
                for i in range(2):
                    turn_pair("w%d" % i, (2, 6)[i], w_t[i])
                turned_pair("SS", "w1")
            if n + 1 < G:
                group_adj("S", n + 1, 1)
            if q == 2:
                group_rows("S", "h0", h_t[0])
            if n < G:
                adj_quant(n, 1)
                da_pass(n, 1, ORDER)
                if q > 0:
                    group_adj("V", n, 0)
                    group_rows("V", "dpJ%d" % (q - 1), dp_t[q - 1])
                adj_quant(n, 0)
                da_pass(n, 0, ORDER)
                group_adj("V", n, 2)
                if q > 0:
                    quant("dpJ%d" % (q - 1), E5M2)
                if q == 0:
                    turned_pair("VV", "w0")
                group_adj("V", n, 3)
                if q == 0:
                    quant("w0", E4M3)
                    quant("w1", E4M3)
                adj_quant(n, 2)
                quant("dpT%d" % q, E5M2, 2, "cdpT")
                adj_quant(n, 3)
                for t in (0, 1):
                    dh(q, t, 2 + t)
                da_pass(n, 2, ORDER)
                da_pass(n, 3, ORDER)
            else:
                group_rows("V", "h1", h_t[1])
                group_rows("V", "dpJ2", dp_t[2])
                quant("h1", E4M3)
                quant("h0", E4M3)
                quant("dpJ2", E5M2)
                group_rows("V", "h2", h_t[2])
                group_rows("V", "dpJ3", dp_t[3])
                quant("h2", E4M3)
                group_rows("S", "h3", h_t[3])
        DW = (4, 5, 0, 1)
        quant("dpT3", E5M2, 2, "cdpT")
        quant("dpJ3", E5M2)
        quant("h3", E4M3)
        for q in range(3):
            for ft in range(4):
                dw(q, ft, DW[ft])
        for t in range(J):
            dh(3, t, (2, 3)[t % 2])
            dh_exit("VS"[t % 2], 3, t)
        for ft in range(4):
            dw(3, ft, DW[ft])
            dw_exit("VS"[ft % 2], ft)
